import numpy as np
import ml_dtypes


def mxq(x, axis, fmt="e4m3"):
    dtype, down = {"e4m3": (ml_dtypes.float8_e4m3fn, 7), "e5m2": (ml_dtypes.float8_e5m2, 14)}[fmt]
    v = np.moveaxis(np.asarray(x, np.float32).astype(ml_dtypes.bfloat16).astype(np.float64), axis, -1)
    blocks = v.reshape(v.shape[:-1] + (-1, 32))
    amax = np.abs(blocks).max(-1, keepdims=True)
    byte = np.maximum(np.where(amax > 0, np.frexp(amax)[1] - 1 + 127, 0) - down, 1)
    scale = np.exp2(byte - 127.0)
    codes = (blocks / scale).astype(np.float32).astype(dtype).astype(np.float64)
    return np.moveaxis((codes * scale).reshape(v.shape), -1, axis)


WIDE = False


def mx_kscale(k):
    if not WIDE:
        return np.ones(k)
    levels = np.array([10, -10, 5, -5, 0])
    a = np.random.permutation(np.resize(levels, k // 512 * 4)).reshape(k // 512, 4)
    idx = np.arange(k)
    return np.exp2(a[idx // 512, idx % 128 // 32])


BF16 = ml_dtypes.bfloat16


def bf(x):
    return np.asarray(x, np.float32).astype(BF16)


def f64(x):
    return np.asarray(x).astype(np.float64)


B, C, S, SEG, HID = 8, 512, 2, 512, 512
LS = S * SEG
R = B * C
ERF_CLIP, ERF_TERMS = 6.0, 120


def erf(v):
    a = np.clip(v, -ERF_CLIP, ERF_CLIP)
    a2 = 2.0 * a * a
    term = a.copy()
    tot = a.copy()
    for n in range(1, ERF_TERMS):
        term = term * a2 / (2.0 * n + 1.0)
        tot = tot + term
    return 2.0 / np.sqrt(np.pi) * np.exp(-a * a) * tot


def gelu_erf(v):
    return 0.5 * v * (1.0 + erf(v / np.sqrt(2.0)))


def setup_inputs():
    sv = np.repeat(mx_kscale(SEG), S)
    return {"x": bf(np.random.standard_normal((B, C, LS)) * sv),
            "wes1": bf(np.random.standard_normal((HID, LS)) / np.sqrt(SEG) / sv),
            "wes2": bf(np.random.standard_normal((LS, S * HID)) * 1.5 / np.sqrt(HID)),
            "wes3": bf(np.random.standard_normal((SEG, LS)) / np.sqrt(S) / sv),
            "bias1": bf(np.random.standard_normal(S * HID) * 0.5),
            "bias2": bf(np.random.standard_normal(LS) * 0.5),
            "bias3": bf(np.random.standard_normal(SEG) * 0.5)}


def reference(x, wes1, wes2, wes3, bias1, bias2, bias3):
    xr = f64(x).reshape(R, SEG, S)
    xs = mxq(xr.transpose(2, 0, 1), 2, "e4m3")
    w1 = mxq(f64(wes1).reshape(HID, SEG, S).transpose(2, 1, 0), 1, "e4m3")
    g = gelu_erf((xs @ w1) + f64(bias1).reshape(S, 1, HID))
    w2r = f64(wes2).reshape(S, SEG, S, HID)
    w2 = np.stack([w2r[i, :, i, :] for i in range(S)]).transpose(0, 2, 1)
    mid = (mxq(g, 2, "e4m3") @ mxq(w2, 1, "e4m3")) + f64(bias2).reshape(S, 1, SEG)
    jj = np.arange(SEG)
    w3 = f64(wes3).reshape(SEG, SEG, S)[jj, jj, :]
    res = (xr * w3).sum(-1) + f64(bias3)
    out = mid + res[None, :, :]
    return out.transpose(1, 2, 0).reshape(B, C, LS)

@@ -1,0 +1,265 @@
+from contextlib import ExitStack
+
+import concourse.mybir as mybir
+from concourse.masks import make_identity
+
+BF16 = mybir.dt.bfloat16
+F32 = mybir.dt.float32
+U32 = mybir.dt.uint32
+U8 = mybir.dt.uint8
+FP8X4 = mybir.dt.float8_e4m3fn_x4
+ADD = mybir.AluOpType.add
+MULT = mybir.AluOpType.mult
+GELU = mybir.ActivationFunctionType.Gelu
+
+P = 128
+PACK = 4
+PHASES = 2
+SEG = 512
+HID = 512
+WIDTH = PHASES * SEG
+ROWS = 8 * 512
+CHUNK = 512
+N_CHUNKS = ROWS // CHUNK
+PIECE = WIDTH // PACK
+FLIPS = CHUNK * PACK // P
+FLIPS_PER_BANK = 8
+HALVES = FLIPS // FLIPS_PER_BANK
+
+FLOPS = 2 * 2 * PHASES * ROWS * SEG * HID + 4 * ROWS * SEG
+BYTES = 2 * (ROWS * WIDTH + HID * WIDTH + PHASES * SEG * HID + 2 * SEG + 2 * WIDTH + SEG) + 4 * ROWS * WIDTH
+
+
+def tile_maskmlp_pa_t_kernel(tc, x, wes1, wes2, wes3, bias1, bias2, bias3, out):
+    nc = tc.nc
+    x_rows = x.rearrange("b c l -> (b c) l")
+    out_rows = out.rearrange("b c l -> (b c) l")
+
+    with ExitStack() as ctx:
+        consts = ctx.enter_context(tc.tile_pool(name="consts", bufs=1))
+        staging = ctx.enter_context(tc.tile_pool(name="staging", bufs=3))
+        double = ctx.enter_context(tc.tile_pool(name="double", bufs=2))
+        triple = ctx.enter_context(tc.tile_pool(name="triple", bufs=3))
+        leaving = ctx.enter_context(tc.tile_pool(name="leaving", bufs=4))
+        psum = ctx.enter_context(tc.psum_pool(name="psum", bufs=2))
+
+        ident_bf = consts.tile([P, P], BF16)
+        make_identity(nc, ident_bf[:])
+        ident_f32 = consts.tile([P, P], F32)
+        make_identity(nc, ident_f32[:])
+
+        warm = consts.tile([P, 1], F32)
+        nc.vector.memset(warm[:], 0.0)
+        nc.scalar.activation(out=warm[:], in_=warm[:], func=GELU)
+
+        def load_rows(rows):
+            pieces = rows.rearrange("r (t w) -> (r t) w", t=PACK).rearrange("(s q) w -> q s w", q=P)
+            staged = staging.tile([P, FLIPS, PIECE], BF16)
+            for half in range(HALVES):
+                tiles = slice(half * FLIPS_PER_BANK, (half + 1) * FLIPS_PER_BANK)
+                nc.sync.dma_start(out=staged[:, tiles, :], in_=pieces[:, tiles, :])
+            return staged
+
+        def flip_and_quantise(staged, codes, scales):
+            by_phase = staged[:].rearrange("q s (j i) -> q s i j", i=PHASES)
+            flat = double.tile([P, PHASES, CHUNK * PACK], BF16, align_bytes=64)
+            for half in range(HALVES):
+                for i in range(PHASES):
+                    flipped = psum.tile([P, FLIPS_PER_BANK * P], BF16, tag="flip")
+                    for s in range(FLIPS_PER_BANK):
+                        nc.tensor.transpose(
+                            out=flipped[:, s * P : (s + 1) * P],
+                            in_=by_phase[:, half * FLIPS_PER_BANK + s, i, :],
+                            identity=ident_bf[:],
+                        )
+                    columns = slice(half * FLIPS_PER_BANK * P, (half + 1) * FLIPS_PER_BANK * P)
+                    nc.scalar.copy(out=flat[:, i, columns], in_=flipped[:])
+            nc.vector.quantize_mx(
+                out=codes.bitcast(FP8X4), scales=scales, in_=flat[:].rearrange("p i c -> p (i c)")
+            )
+            return flat
+
+        w1_staged = load_rows(wes1)
+        x_staged = {0: load_rows(x_rows[0:CHUNK, :])}
+
+        small_rows = consts.tile([P, P], BF16)
+        nc.vector.memset(small_rows[:], 0.0)
+        nc.scalar.dma_start(out=small_rows[0:8, :], in_=bias1.rearrange("(a p) -> a p", p=P))
+        nc.scalar.dma_start(out=small_rows[8:16, :], in_=bias2.rearrange("(a p) -> a p", p=P))
+        nc.scalar.dma_start(out=small_rows[16:20, :], in_=bias3.rearrange("(a p) -> a p", p=P))
+        w3_pairs = wes3.rearrange("j (jj k) -> (j jj) k", k=PHASES)[0 : SEG * SEG : SEG + 1, :]
+        w3_bf = consts.tile([P, PACK, PHASES], BF16)
+        nc.scalar.dma_start(out=w3_bf[:], in_=w3_pairs.rearrange("(t p) k -> p t k", p=P))
+
+        w2_staged = consts.tile([P, PHASES, PACK, HID], BF16)
+        for i in range(PHASES):
+            block = wes2[i * SEG : (i + 1) * SEG, i * HID : (i + 1) * HID]
+            nc.sync.dma_start(out=w2_staged[:, i, :, :], in_=block.rearrange("(t p) h -> p t h", p=P))
+        x_staged[1] = load_rows(x_rows[CHUNK : 2 * CHUNK, :])
+
+        small_ps = psum.tile([P, P], BF16, tag="flip")
+        nc.tensor.transpose(out=small_ps[:], in_=small_rows[:], identity=ident_bf[:])
+        small_cols = consts.tile([P, 20], F32)
+        nc.vector.tensor_copy(out=small_cols[:], in_=small_ps[:, 0:20])
+        bias1_col = small_cols[:, 0:8]
+        bias23_col = consts.tile([P, PHASES * PACK], F32)
+        for i in range(PHASES):
+            nc.vector.tensor_add(
+                out=bias23_col[:, i * PACK : (i + 1) * PACK],
+                in0=small_cols[:, 8 + i * PACK : 8 + (i + 1) * PACK],
+                in1=small_cols[:, 16:20],
+            )
+        w3_col = consts.tile([P, PACK * PHASES], F32)
+        nc.vector.tensor_copy(out=w3_col[:], in_=w3_bf[:].rearrange("p t k -> p (t k)"))
+
+        x_grouped, x_codes, x_scales, res_t = {}, {}, {}, {}
+        g_rows, g_grouped, g_codes, g_scales, sum_t = {}, {}, {}, {}, {}
+
+        def flip_chunk(c):
+            xq = double.tile([P, PHASES * CHUNK], U32, align_bytes=64)
+            xs = double.tile([P, PHASES * CHUNK], U8, align_bytes=64)
+            x_grouped[c] = flip_and_quantise(x_staged[c], xq[:], xs[:])
+            x_codes[c], x_scales[c] = xq, xs
+
+        def residual(c):
+            by_tile = x_grouped[c][:].rearrange("p i (r t) -> p i t r", t=PACK)
+            odd = double.tile([P, PACK, CHUNK], F32)
+            res = triple.tile([P, PACK, CHUNK], F32)
+            for t in range(PACK):
+                nc.vector.tensor_scalar(
+                    out=odd[:, t, :], in0=by_tile[:, 1, t, :],
+                    scalar1=w3_col[:, 2 * t + 1 : 2 * t + 2], scalar2=None, op0=MULT,
+                )
+            for t in range(PACK):
+                nc.vector.scalar_tensor_tensor(
+                    out=res[:, t, :], in0=by_tile[:, 0, t, :], scalar=w3_col[:, 2 * t : 2 * t + 1],
+                    in1=odd[:, t, :], op0=MULT, op1=ADD,
+                )
+            res_t[c] = res
+
+        def first_matmul(c, i, t):
+            if i == 0 and t == 0:
+                rows = double.tile([P, PHASES, PACK, CHUNK], BF16)
+                g_rows[c] = rows
+            units = slice(i * HID + t * P, i * HID + (t + 1) * P)
+            columns = slice(i * CHUNK, (i + 1) * CHUNK)
+            hidden_ps = psum.tile([P, CHUNK], F32, tag="hidden")
+            nc.tensor.matmul_mx(
+                out=hidden_ps[:],
+                lhsT=w1_codes[:, units].bitcast(FP8X4), lhsT_scale=w1_scales[:, units],
+                rhs=x_codes[c][:, columns].bitcast(FP8X4), rhs_scale=x_scales[c][:, columns],
+                start=True, stop=True,
+            )
+            nc.scalar.activation(
+                out=g_rows[c][:, i, t, :], in_=hidden_ps[:], func=GELU,
+                bias=bias1_col[:, i * PACK + t : i * PACK + t + 1], scale=1.0,
+            )
+
+        def group_g(c, i):
+            if i == 0:
+                grouped = double.tile([P, PHASES, CHUNK * PACK], BF16, align_bytes=64)
+                g_grouped[c] = grouped
+            nc.vector.tensor_copy(
+                out=g_grouped[c][:, i, :].rearrange("p (c u t) -> p c t u", u=4, t=PACK),
+                in_=g_rows[c][:, i, :, :].rearrange("p t (c u) -> p c t u", u=4),
+            )
+
+        def quantise_g(c, i):
+            if i == 0:
+                gq = double.tile([P, PHASES * CHUNK], U32, align_bytes=64)
+                gs = double.tile([P, PHASES * CHUNK], U8, align_bytes=64)
+                g_codes[c], g_scales[c] = gq, gs
+            columns = slice(i * CHUNK, (i + 1) * CHUNK)
+            nc.vector.quantize_mx(
+                out=g_codes[c][:, columns].bitcast(FP8X4), scales=g_scales[c][:, columns],
+                in_=g_grouped[c][:, i, :],
+            )
+
+        def second_matmul(c, i, t):
+            if i == 0 and t == 0:
+                sums = double.tile([P, PHASES, PACK, CHUNK], F32)
+                sum_t[c] = sums
+            outputs = slice(i * SEG + t * P, i * SEG + (t + 1) * P)
+            columns = slice(i * CHUNK, (i + 1) * CHUNK)
+            mixed_ps = psum.tile([P, CHUNK], F32, tag="mixed")
+            nc.tensor.matmul_mx(
+                out=mixed_ps[:],
+                lhsT=w2_codes[:, outputs].bitcast(FP8X4), lhsT_scale=w2_scales[:, outputs],
+                rhs=g_codes[c][:, columns].bitcast(FP8X4), rhs_scale=g_scales[c][:, columns],
+                start=True, stop=True,
+            )
+            nc.vector.scalar_tensor_tensor(
+                out=sum_t[c][:, i, t, :], in0=mixed_ps[:],
+                scalar=bias23_col[:, i * PACK + t : i * PACK + t + 1],
+                in1=res_t[c][:, t, :], op0=ADD, op1=ADD,
+            )
+
+        def bring_back(c):
+            for a in range(CHUNK // P):
+                rows_out = leaving.tile([P, WIDTH], F32)
+                for half in range(2):
+                    back_ps = psum.tile([P, PHASES, 2, P], F32, tag="back")
+                    for i in range(PHASES):
+                        for t in range(2):
+                            nc.tensor.transpose(
+                                out=back_ps[:, i, t, :],
+                                in_=sum_t[c][:, i, 2 * half + t, a * P : (a + 1) * P],
+                                identity=ident_f32[:],
+                            )
+                    nc.scalar.copy(
+                        out=rows_out[:, half * SEG : (half + 1) * SEG].rearrange("p (j i) -> p j i", i=PHASES),
+                        in_=back_ps[:].rearrange("p i t j -> p (t j) i"),
+                    )
+                first_row = c * CHUNK + a * P
+                nc.gpsimd.dma_start(out=out_rows[first_row : first_row + P, :], in_=rows_out[:])
+
+        w1_codes = consts.tile([P, PHASES * HID], U32, align_bytes=64)
+        w1_scales = consts.tile([P, PHASES * HID], U8, align_bytes=64)
+        flip_and_quantise(w1_staged, w1_codes[:], w1_scales[:])
+        x_staged[2] = load_rows(x_rows[2 * CHUNK : 3 * CHUNK, :])
+        flip_chunk(0)
+        residual(0)
+
+        w2_grouped = consts.tile([P, PHASES, SEG, PACK], BF16, align_bytes=64)
+        for i in range(PHASES):
+            for half in range(2):
+                w2_ps = psum.tile([P, 2, PACK, P], BF16, tag="flip")
+                for b in range(2):
+                    for t in range(PACK):
+                        nc.tensor.transpose(
+                            out=w2_ps[:, b, t, :],
+                            in_=w2_staged[:, i, 2 * half + b, t * P : (t + 1) * P],
+                            identity=ident_bf[:],
+                        )
+                nc.vector.tensor_copy(
+                    out=w2_grouped[:, i, half * 2 * P : (half + 1) * 2 * P, :].rearrange("p (b j) t -> p b j t", b=2),
+                    in_=w2_ps[:].rearrange("p b t j -> p b j t"),
+                )
+        w2_codes = consts.tile([P, PHASES * SEG], U32, align_bytes=64)
+        w2_scales = consts.tile([P, PHASES * SEG], U8, align_bytes=64)
+        nc.vector.quantize_mx(
+            out=w2_codes[:].bitcast(FP8X4), scales=w2_scales[:],
+            in_=w2_grouped[:].rearrange("p i j t -> p (i j t)"),
+        )
+
+        for k in range(1, N_CHUNKS + 3):
+            if k + 2 < N_CHUNKS:
+                x_staged[k + 2] = load_rows(x_rows[(k + 2) * CHUNK : (k + 3) * CHUNK, :])
+            if k < N_CHUNKS:
+                flip_chunk(k)
+            if k >= 3:
+                bring_back(k - 3)
+            for i in range(PHASES):
+                for t in range(PACK):
+                    if k - 1 < N_CHUNKS:
+                        first_matmul(k - 1, i, t)
+                    if 0 <= k - 2 < N_CHUNKS:
+                        second_matmul(k - 2, i, t)
+                if k - 1 < N_CHUNKS:
+                    group_g(k - 1, i)
+                    if i == 1:
+                        quantise_g(k - 1, 0)
+            if k < N_CHUNKS:
+                residual(k)
+            if k - 1 < N_CHUNKS:
+                quantise_g(k - 1, 1)

@@ -211,7 +211,7 @@ def tile_maskmlp_pa_t_kernel(tc, x, wes1, wes2, wes3, bias1, bias2, bias3, out):
                         in_=back_ps[:].rearrange("p i t j -> p (t j) i"),
                     )
                 first_row = c * CHUNK + a * P
-                nc.gpsimd.dma_start(out=out_rows[first_row : first_row + P, :], in_=rows_out[:])
+                nc.sync.dma_start(out=out_rows[first_row : first_row + P, :], in_=rows_out[:])
 
         w1_codes = consts.tile([P, PHASES * HID], U32, align_bytes=64)
         w1_scales = consts.tile([P, PHASES * HID], U8, align_bytes=64)

@@ -26,6 +26,8 @@ FLIPS = CHUNK * PACK // P
 FLIPS_PER_BANK = 8
 HALVES = FLIPS // FLIPS_PER_BANK
 
+DIAGONALS = ((0, 1), (1, 1), (2, 1))
+
 FLOPS = 2 * 2 * PHASES * ROWS * SEG * HID + 4 * ROWS * SEG
 BYTES = 2 * (ROWS * WIDTH + HID * WIDTH + PHASES * SEG * HID + 2 * SEG + 2 * WIDTH + SEG) + 4 * ROWS * WIDTH
 
@@ -40,6 +42,7 @@ def tile_maskmlp_pa_t_kernel(tc, x, wes1, wes2, wes3, bias1, bias2, bias3, out):
         staging = ctx.enter_context(tc.tile_pool(name="staging", bufs=3))
         double = ctx.enter_context(tc.tile_pool(name="double", bufs=2))
         triple = ctx.enter_context(tc.tile_pool(name="triple", bufs=3))
+        lasting = ctx.enter_context(tc.tile_pool(name="lasting", bufs=5))
         leaving = ctx.enter_context(tc.tile_pool(name="leaving", bufs=4))
         psum = ctx.enter_context(tc.psum_pool(name="psum", bufs=2))
 
@@ -62,7 +65,7 @@ def tile_maskmlp_pa_t_kernel(tc, x, wes1, wes2, wes3, bias1, bias2, bias3, out):
 
         def flip_and_quantise(staged, codes, scales):
             by_phase = staged[:].rearrange("q s (j i) -> q s i j", i=PHASES)
-            flat = double.tile([P, PHASES, CHUNK * PACK], BF16, align_bytes=64)
+            flat = lasting.tile([P, PHASES, CHUNK * PACK], BF16, align_bytes=64)
             for half in range(HALVES):
                 for i in range(PHASES):
                     flipped = psum.tile([P, FLIPS_PER_BANK * P], BF16, tag="flip")
@@ -112,6 +115,16 @@ def tile_maskmlp_pa_t_kernel(tc, x, wes1, wes2, wes3, bias1, bias2, bias3, out):
         w3_col = consts.tile([P, PACK * PHASES], F32)
         nc.vector.tensor_copy(out=w3_col[:], in_=w3_bf[:].rearrange("p t k -> p (t k)"))
 
+        diagonals = {}
+        for t, k in DIAGONALS:
+            diagonal = consts.tile([P, PHASES, P], BF16, name="diagonal_%d_%d" % (t, k))
+            for i in range(PHASES):
+                nc.vector.tensor_scalar(
+                    out=diagonal[:, i, :], in0=ident_bf[:],
+                    scalar1=w3_col[:, 2 * t + k : 2 * t + k + 1], scalar2=None, op0=MULT,
+                )
+            diagonals[t, k] = diagonal
+
         x_grouped, x_codes, x_scales, res_t = {}, {}, {}, {}
         g_rows, g_grouped, g_codes, g_scales, sum_t = {}, {}, {}, {}, {}
 
@@ -126,15 +139,22 @@ def tile_maskmlp_pa_t_kernel(tc, x, wes1, wes2, wes3, bias1, bias2, bias3, out):
             odd = double.tile([P, PACK, CHUNK], F32)
             res = triple.tile([P, PACK, CHUNK], F32)
             for t in range(PACK):
-                nc.vector.tensor_scalar(
-                    out=odd[:, t, :], in0=by_tile[:, 1, t, :],
-                    scalar1=w3_col[:, 2 * t + 1 : 2 * t + 2], scalar2=None, op0=MULT,
-                )
+                if (t, 1) not in DIAGONALS:
+                    nc.vector.tensor_scalar(
+                        out=odd[:, t, :], in0=by_tile[:, 1, t, :],
+                        scalar1=w3_col[:, 2 * t + 1 : 2 * t + 2], scalar2=None, op0=MULT,
+                    )
             for t in range(PACK):
-                nc.vector.scalar_tensor_tensor(
-                    out=res[:, t, :], in0=by_tile[:, 0, t, :], scalar=w3_col[:, 2 * t : 2 * t + 1],
-                    in1=odd[:, t, :], op0=MULT, op1=ADD,
-                )
+                if (t, 1) not in DIAGONALS:
+                    nc.vector.scalar_tensor_tensor(
+                        out=res[:, t, :], in0=by_tile[:, 0, t, :], scalar=w3_col[:, 2 * t : 2 * t + 1],
+                        in1=odd[:, t, :], op0=MULT, op1=ADD,
+                    )
+                elif (t, 0) not in DIAGONALS:
+                    nc.vector.tensor_scalar(
+                        out=res[:, t, :], in0=by_tile[:, 0, t, :],
+                        scalar1=w3_col[:, 2 * t : 2 * t + 1], scalar2=None, op0=MULT,
+                    )
             res_t[c] = res
 
         def first_matmul(c, i, t):
@@ -188,24 +208,39 @@ def tile_maskmlp_pa_t_kernel(tc, x, wes1, wes2, wes3, bias1, bias2, bias3, out):
                 rhs=g_codes[c][:, columns].bitcast(FP8X4), rhs_scale=g_scales[c][:, columns],
                 start=True, stop=True,
             )
-            nc.vector.scalar_tensor_tensor(
-                out=sum_t[c][:, i, t, :], in0=mixed_ps[:],
-                scalar=bias23_col[:, i * PACK + t : i * PACK + t + 1],
-                in1=res_t[c][:, t, :], op0=ADD, op1=ADD,
-            )
+            bias = bias23_col[:, i * PACK + t : i * PACK + t + 1]
+            if (t, 0) in DIAGONALS and (t, 1) in DIAGONALS:
+                nc.vector.tensor_scalar(
+                    out=sum_t[c][:, i, t, :], in0=mixed_ps[:], scalar1=bias, scalar2=None, op0=ADD,
+                )
+            else:
+                nc.vector.scalar_tensor_tensor(
+                    out=sum_t[c][:, i, t, :], in0=mixed_ps[:], scalar=bias,
+                    in1=res_t[c][:, t, :], op0=ADD, op1=ADD,
+                )
 
         def bring_back(c):
             for a in range(CHUNK // P):
                 rows_out = leaving.tile([P, WIDTH], F32)
                 for half in range(2):
                     back_ps = psum.tile([P, PHASES, 2, P], F32, tag="back")
-                    for i in range(PHASES):
-                        for t in range(2):
-                            nc.tensor.transpose(
-                                out=back_ps[:, i, t, :],
-                                in_=sum_t[c][:, i, 2 * half + t, a * P : (a + 1) * P],
-                                identity=ident_f32[:],
-                            )
+                    tiles = (2 * half, 2 * half + 1)
+                    adds = [(t, k) for t, k in DIAGONALS if t in tiles]
+                    for n, (i, t) in enumerate((i, t) for i in range(PHASES) for t in tiles):
+                        nc.tensor.matmul(
+                            out=back_ps[:, i, t - tiles[0], :],
+                            lhsT=sum_t[c][:, i, t, a * P : (a + 1) * P],
+                            rhs=ident_f32[:], is_transpose=True,
+                            start=n == 0 or not adds, stop=not adds,
+                        )
+                    by_tile = x_grouped[c][:].rearrange("p i (r t) -> p i t r", t=PACK)
+                    for n, (t, k) in enumerate(adds):
+                        nc.tensor.matmul(
+                            out=back_ps[:, :, t - tiles[0], :],
+                            lhsT=by_tile[:, k, t, a * P : (a + 1) * P],
+                            rhs=diagonals[t, k][:],
+                            start=False, stop=n == len(adds) - 1,
+                        )
                     nc.scalar.copy(
                         out=rows_out[:, half * SEG : (half + 1) * SEG].rearrange("p (j i) -> p j i", i=PHASES),
                         in_=back_ps[:].rearrange("p i t j -> p (t j) i"),

@@ -20,13 +20,18 @@ HID = 512
 WIDTH = PHASES * SEG
 ROWS = 8 * 512
 CHUNK = 512
-N_CHUNKS = ROWS // CHUNK
+CHUNKS = (CHUNK // 2,) + (CHUNK,) * (ROWS // CHUNK - 1) + (CHUNK // 2,)
+FIRST_ROWS = tuple(sum(CHUNKS[:c]) for c in range(len(CHUNKS)))
+N_CHUNKS = len(CHUNKS)
 PIECE = WIDTH // PACK
-FLIPS = CHUNK * PACK // P
 FLIPS_PER_BANK = 8
-HALVES = FLIPS // FLIPS_PER_BANK
+BANK_ROWS = FLIPS_PER_BANK * P // PACK
 
-DIAGONALS = ((0, 1), (1, 1), (2, 1))
+DIAGONALS = ((0, 1), (1, 1))
+
+FLIP_TO_FIRST = 1
+FIRST_TO_SECOND = 2
+SECOND_TO_BACK = 1
 
 FLOPS = 2 * 2 * PHASES * ROWS * SEG * HID + 4 * ROWS * SEG
 BYTES = 2 * (ROWS * WIDTH + HID * WIDTH + PHASES * SEG * HID + 2 * SEG + 2 * WIDTH + SEG) + 4 * ROWS * WIDTH
@@ -57,33 +62,29 @@ def tile_maskmlp_pa_t_kernel(tc, x, wes1, wes2, wes3, bias1, bias2, bias3, out):
 
         def load_rows(rows):
             pieces = rows.rearrange("r (t w) -> (r t) w", t=PACK).rearrange("(s q) w -> q s w", q=P)
-            staged = staging.tile([P, FLIPS, PIECE], BF16)
-            for half in range(HALVES):
-                tiles = slice(half * FLIPS_PER_BANK, (half + 1) * FLIPS_PER_BANK)
-                nc.sync.dma_start(out=staged[:, tiles, :], in_=pieces[:, tiles, :])
+            n_tiles = rows.shape[0] * PACK // P
+            staged = staging.tile([P, n_tiles, PIECE], BF16)
+            for s in range(0, n_tiles, FLIPS_PER_BANK):
+                nc.sync.dma_start(out=staged[:, s : s + FLIPS_PER_BANK, :], in_=pieces[:, s : s + FLIPS_PER_BANK, :])
             return staged
 
-        def flip_and_quantise(staged, codes, scales):
+        def flip_bank(staged, flat, b, i, copy):
             by_phase = staged[:].rearrange("q s (j i) -> q s i j", i=PHASES)
-            flat = lasting.tile([P, PHASES, CHUNK * PACK], BF16, align_bytes=64)
-            for half in range(HALVES):
-                for i in range(PHASES):
-                    flipped = psum.tile([P, FLIPS_PER_BANK * P], BF16, tag="flip")
-                    for s in range(FLIPS_PER_BANK):
-                        nc.tensor.transpose(
-                            out=flipped[:, s * P : (s + 1) * P],
-                            in_=by_phase[:, half * FLIPS_PER_BANK + s, i, :],
-                            identity=ident_bf[:],
-                        )
-                    columns = slice(half * FLIPS_PER_BANK * P, (half + 1) * FLIPS_PER_BANK * P)
-                    nc.scalar.copy(out=flat[:, i, columns], in_=flipped[:])
-            nc.vector.quantize_mx(
-                out=codes.bitcast(FP8X4), scales=scales, in_=flat[:].rearrange("p i c -> p (i c)")
-            )
-            return flat
+            flipped = psum.tile([P, FLIPS_PER_BANK * P], BF16, tag="flip")
+            for s in range(FLIPS_PER_BANK):
+                nc.tensor.transpose(
+                    out=flipped[:, s * P : (s + 1) * P],
+                    in_=by_phase[:, b * FLIPS_PER_BANK + s, i, :],
+                    identity=ident_bf[:],
+                )
+            columns = slice(b * FLIPS_PER_BANK * P, (b + 1) * FLIPS_PER_BANK * P)
+            copy(out=flat[:, i, columns], in_=flipped[:])
 
+        def load_chunk(c):
+            return load_rows(x_rows[FIRST_ROWS[c] : FIRST_ROWS[c] + CHUNKS[c], :])
+
+        x_staged = {0: load_chunk(0)}
         w1_staged = load_rows(wes1)
-        x_staged = {0: load_rows(x_rows[0:CHUNK, :])}
 
         small_rows = consts.tile([P, P], BF16)
         nc.vector.memset(small_rows[:], 0.0)
@@ -94,11 +95,11 @@ def tile_maskmlp_pa_t_kernel(tc, x, wes1, wes2, wes3, bias1, bias2, bias3, out):
         w3_bf = consts.tile([P, PACK, PHASES], BF16)
         nc.scalar.dma_start(out=w3_bf[:], in_=w3_pairs.rearrange("(t p) k -> p t k", p=P))
 
+        x_staged[1] = load_chunk(1)
         w2_staged = consts.tile([P, PHASES, PACK, HID], BF16)
         for i in range(PHASES):
             block = wes2[i * SEG : (i + 1) * SEG, i * HID : (i + 1) * HID]
             nc.sync.dma_start(out=w2_staged[:, i, :, :], in_=block.rearrange("(t p) h -> p t h", p=P))
-        x_staged[1] = load_rows(x_rows[CHUNK : 2 * CHUNK, :])
 
         small_ps = psum.tile([P, P], BF16, tag="flip")
         nc.tensor.transpose(out=small_ps[:], in_=small_rows[:], identity=ident_bf[:])
@@ -128,42 +129,53 @@ def tile_maskmlp_pa_t_kernel(tc, x, wes1, wes2, wes3, bias1, bias2, bias3, out):
         x_grouped, x_codes, x_scales, res_t = {}, {}, {}, {}
         g_rows, g_grouped, g_codes, g_scales, sum_t = {}, {}, {}, {}, {}
 
-        def flip_chunk(c):
-            xq = double.tile([P, PHASES * CHUNK], U32, align_bytes=64)
-            xs = double.tile([P, PHASES * CHUNK], U8, align_bytes=64)
-            x_grouped[c] = flip_and_quantise(x_staged[c], xq[:], xs[:])
-            x_codes[c], x_scales[c] = xq, xs
+        def open_chunk(c):
+            flat = lasting.tile([P, PHASES, CHUNKS[c] * PACK], BF16, align_bytes=64)
+            xq = double.tile([P, PHASES * CHUNKS[c]], U32, align_bytes=64)
+            xs = double.tile([P, PHASES * CHUNKS[c]], U8, align_bytes=64)
+            x_grouped[c], x_codes[c], x_scales[c] = flat, xq, xs
 
-        def residual(c):
+        def flip(c, i, b):
+            if i == 0 and b == 0:
+                open_chunk(c)
+            flip_bank(x_staged[c], x_grouped[c], b, i, nc.scalar.copy)
+            if (b + 1) * BANK_ROWS == CHUNKS[c]:
+                columns = slice(i * CHUNKS[c], (i + 1) * CHUNKS[c])
+                nc.vector.quantize_mx(
+                    out=x_codes[c][:, columns].bitcast(FP8X4), scales=x_scales[c][:, columns],
+                    in_=x_grouped[c][:, i, :],
+                )
+                if i == 1 and c + 2 < N_CHUNKS:
+                    x_staged[c + 2] = load_chunk(c + 2)
+
+        def residual(c, t):
+            if t == 0:
+                res = triple.tile([P, PACK, CHUNKS[c]], F32)
+                res_t[c] = res
             by_tile = x_grouped[c][:].rearrange("p i (r t) -> p i t r", t=PACK)
-            odd = double.tile([P, PACK, CHUNK], F32)
-            res = triple.tile([P, PACK, CHUNK], F32)
-            for t in range(PACK):
-                if (t, 1) not in DIAGONALS:
-                    nc.vector.tensor_scalar(
-                        out=odd[:, t, :], in0=by_tile[:, 1, t, :],
-                        scalar1=w3_col[:, 2 * t + 1 : 2 * t + 2], scalar2=None, op0=MULT,
-                    )
-            for t in range(PACK):
-                if (t, 1) not in DIAGONALS:
-                    nc.vector.scalar_tensor_tensor(
-                        out=res[:, t, :], in0=by_tile[:, 0, t, :], scalar=w3_col[:, 2 * t : 2 * t + 1],
-                        in1=odd[:, t, :], op0=MULT, op1=ADD,
-                    )
-                elif (t, 0) not in DIAGONALS:
-                    nc.vector.tensor_scalar(
-                        out=res[:, t, :], in0=by_tile[:, 0, t, :],
-                        scalar1=w3_col[:, 2 * t : 2 * t + 1], scalar2=None, op0=MULT,
-                    )
-            res_t[c] = res
+            w3_even = w3_col[:, 2 * t : 2 * t + 1]
+            if (t, 1) in DIAGONALS:
+                nc.vector.tensor_scalar(
+                    out=res_t[c][:, t, :], in0=by_tile[:, 0, t, :], scalar1=w3_even, scalar2=None, op0=MULT,
+                )
+            else:
+                odd = triple.tile([P, CHUNKS[c]], F32)
+                nc.vector.tensor_scalar(
+                    out=odd[:], in0=by_tile[:, 1, t, :],
+                    scalar1=w3_col[:, 2 * t + 1 : 2 * t + 2], scalar2=None, op0=MULT,
+                )
+                nc.vector.scalar_tensor_tensor(
+                    out=res_t[c][:, t, :], in0=by_tile[:, 0, t, :], scalar=w3_even,
+                    in1=odd[:], op0=MULT, op1=ADD,
+                )
 
         def first_matmul(c, i, t):
             if i == 0 and t == 0:
-                rows = double.tile([P, PHASES, PACK, CHUNK], BF16)
+                rows = double.tile([P, PHASES, PACK, CHUNKS[c]], BF16)
                 g_rows[c] = rows
             units = slice(i * HID + t * P, i * HID + (t + 1) * P)
-            columns = slice(i * CHUNK, (i + 1) * CHUNK)
-            hidden_ps = psum.tile([P, CHUNK], F32, tag="hidden")
+            columns = slice(i * CHUNKS[c], (i + 1) * CHUNKS[c])
+            hidden_ps = psum.tile([P, CHUNKS[c]], F32, tag="hidden")
             nc.tensor.matmul_mx(
                 out=hidden_ps[:],
                 lhsT=w1_codes[:, units].bitcast(FP8X4), lhsT_scale=w1_scales[:, units],
@@ -177,7 +189,7 @@ def tile_maskmlp_pa_t_kernel(tc, x, wes1, wes2, wes3, bias1, bias2, bias3, out):
 
         def group_g(c, i):
             if i == 0:
-                grouped = double.tile([P, PHASES, CHUNK * PACK], BF16, align_bytes=64)
+                grouped = double.tile([P, PHASES, CHUNKS[c] * PACK], BF16, align_bytes=64)
                 g_grouped[c] = grouped
             nc.vector.tensor_copy(
                 out=g_grouped[c][:, i, :].rearrange("p (c u t) -> p c t u", u=4, t=PACK),
@@ -186,10 +198,10 @@ def tile_maskmlp_pa_t_kernel(tc, x, wes1, wes2, wes3, bias1, bias2, bias3, out):
 
         def quantise_g(c, i):
             if i == 0:
-                gq = double.tile([P, PHASES * CHUNK], U32, align_bytes=64)
-                gs = double.tile([P, PHASES * CHUNK], U8, align_bytes=64)
+                gq = double.tile([P, PHASES * CHUNKS[c]], U32, align_bytes=64)
+                gs = double.tile([P, PHASES * CHUNKS[c]], U8, align_bytes=64)
                 g_codes[c], g_scales[c] = gq, gs
-            columns = slice(i * CHUNK, (i + 1) * CHUNK)
+            columns = slice(i * CHUNKS[c], (i + 1) * CHUNKS[c])
             nc.vector.quantize_mx(
                 out=g_codes[c][:, columns].bitcast(FP8X4), scales=g_scales[c][:, columns],
                 in_=g_grouped[c][:, i, :],
@@ -197,11 +209,11 @@ def tile_maskmlp_pa_t_kernel(tc, x, wes1, wes2, wes3, bias1, bias2, bias3, out):
 
         def second_matmul(c, i, t):
             if i == 0 and t == 0:
-                sums = double.tile([P, PHASES, PACK, CHUNK], F32)
+                sums = double.tile([P, PHASES, PACK, CHUNKS[c]], F32)
                 sum_t[c] = sums
             outputs = slice(i * SEG + t * P, i * SEG + (t + 1) * P)
-            columns = slice(i * CHUNK, (i + 1) * CHUNK)
-            mixed_ps = psum.tile([P, CHUNK], F32, tag="mixed")
+            columns = slice(i * CHUNKS[c], (i + 1) * CHUNKS[c])
+            mixed_ps = psum.tile([P, CHUNKS[c]], F32, tag="mixed")
             nc.tensor.matmul_mx(
                 out=mixed_ps[:],
                 lhsT=w2_codes[:, outputs].bitcast(FP8X4), lhsT_scale=w2_scales[:, outputs],
@@ -209,55 +221,46 @@ def tile_maskmlp_pa_t_kernel(tc, x, wes1, wes2, wes3, bias1, bias2, bias3, out):
                 start=True, stop=True,
             )
             bias = bias23_col[:, i * PACK + t : i * PACK + t + 1]
-            if (t, 0) in DIAGONALS and (t, 1) in DIAGONALS:
-                nc.vector.tensor_scalar(
-                    out=sum_t[c][:, i, t, :], in0=mixed_ps[:], scalar1=bias, scalar2=None, op0=ADD,
-                )
-            else:
-                nc.vector.scalar_tensor_tensor(
-                    out=sum_t[c][:, i, t, :], in0=mixed_ps[:], scalar=bias,
-                    in1=res_t[c][:, t, :], op0=ADD, op1=ADD,
-                )
+            nc.vector.scalar_tensor_tensor(
+                out=sum_t[c][:, i, t, :], in0=mixed_ps[:], scalar=bias,
+                in1=res_t[c][:, t, :], op0=ADD, op1=ADD,
+            )
 
-        def bring_back(c):
-            for a in range(CHUNK // P):
-                rows_out = leaving.tile([P, WIDTH], F32)
-                for half in range(2):
-                    back_ps = psum.tile([P, PHASES, 2, P], F32, tag="back")
-                    tiles = (2 * half, 2 * half + 1)
-                    adds = [(t, k) for t, k in DIAGONALS if t in tiles]
-                    for n, (i, t) in enumerate((i, t) for i in range(PHASES) for t in tiles):
+        def bring_back(c, a, tag):
+            rows_out = leaving.tile([P, WIDTH], F32)
+            by_tile = x_grouped[c][:].rearrange("p i (r t) -> p i t r", t=PACK)
+            rows = slice(a * P, (a + 1) * P)
+            banks = []
+            for half in range(2):
+                back_ps = psum.tile([P, PHASES, 2, P], F32, name="back_ps", tag=tag)
+                banks.append(back_ps)
+                adds = any(t // 2 == half for t, k in DIAGONALS)
+                for i in range(PHASES):
+                    for t in range(2):
                         nc.tensor.matmul(
-                            out=back_ps[:, i, t - tiles[0], :],
-                            lhsT=sum_t[c][:, i, t, a * P : (a + 1) * P],
+                            out=back_ps[:, i, t, :], lhsT=sum_t[c][:, i, 2 * half + t, rows],
                             rhs=ident_f32[:], is_transpose=True,
-                            start=n == 0 or not adds, stop=not adds,
+                            start=not adds or (i == 0 and t == 0), stop=not adds,
                         )
-                    by_tile = x_grouped[c][:].rearrange("p i (r t) -> p i t r", t=PACK)
-                    for n, (t, k) in enumerate(adds):
-                        nc.tensor.matmul(
-                            out=back_ps[:, :, t - tiles[0], :],
-                            lhsT=by_tile[:, k, t, a * P : (a + 1) * P],
-                            rhs=diagonals[t, k][:],
-                            start=False, stop=n == len(adds) - 1,
-                        )
-                    nc.scalar.copy(
-                        out=rows_out[:, half * SEG : (half + 1) * SEG].rearrange("p (j i) -> p j i", i=PHASES),
-                        in_=back_ps[:].rearrange("p i t j -> p (t j) i"),
-                    )
-                first_row = c * CHUNK + a * P
-                nc.sync.dma_start(out=out_rows[first_row : first_row + P, :], in_=rows_out[:])
-
-        w1_codes = consts.tile([P, PHASES * HID], U32, align_bytes=64)
-        w1_scales = consts.tile([P, PHASES * HID], U8, align_bytes=64)
-        flip_and_quantise(w1_staged, w1_codes[:], w1_scales[:])
-        x_staged[2] = load_rows(x_rows[2 * CHUNK : 3 * CHUNK, :])
-        flip_chunk(0)
-        residual(0)
+            for t, k in DIAGONALS:
+                nc.tensor.matmul(
+                    out=banks[t // 2][:, :, t % 2, :], lhsT=by_tile[:, k, t, rows], rhs=diagonals[t, k][:],
+                    start=False, stop=(t, k) == max(d for d in DIAGONALS if d[0] // 2 == t // 2),
+                )
+            for half in range(2):
+                nc.scalar.copy(
+                    out=rows_out[:, half * SEG : (half + 1) * SEG].rearrange("p (j i) -> p j i", i=PHASES),
+                    in_=banks[half][:].rearrange("p i t j -> p (t j) i"),
+                )
+            first_row = FIRST_ROWS[c] + a * P
+            nc.sync.dma_start(out=out_rows[first_row : first_row + P, :], in_=rows_out[:])
 
         w2_grouped = consts.tile([P, PHASES, SEG, PACK], BF16, align_bytes=64)
-        for i in range(PHASES):
-            for half in range(2):
+        w2_codes = consts.tile([P, PHASES * SEG], U32, align_bytes=64)
+        w2_scales = consts.tile([P, PHASES * SEG], U8, align_bytes=64)
+
+        def flip_w2(i):
+            for half, copy in enumerate((nc.scalar.copy, nc.vector.tensor_copy)):
                 w2_ps = psum.tile([P, 2, PACK, P], BF16, tag="flip")
                 for b in range(2):
                     for t in range(PACK):
@@ -266,35 +269,80 @@ def tile_maskmlp_pa_t_kernel(tc, x, wes1, wes2, wes3, bias1, bias2, bias3, out):
                             in_=w2_staged[:, i, 2 * half + b, t * P : (t + 1) * P],
                             identity=ident_bf[:],
                         )
-                nc.vector.tensor_copy(
+                copy(
                     out=w2_grouped[:, i, half * 2 * P : (half + 1) * 2 * P, :].rearrange("p (b j) t -> p b j t", b=2),
                     in_=w2_ps[:].rearrange("p b t j -> p b j t"),
                 )
-        w2_codes = consts.tile([P, PHASES * SEG], U32, align_bytes=64)
-        w2_scales = consts.tile([P, PHASES * SEG], U8, align_bytes=64)
-        nc.vector.quantize_mx(
-            out=w2_codes[:].bitcast(FP8X4), scales=w2_scales[:],
-            in_=w2_grouped[:].rearrange("p i j t -> p (i j t)"),
-        )
+            columns = slice(i * SEG, (i + 1) * SEG)
+            nc.vector.quantize_mx(
+                out=w2_codes[:, columns].bitcast(FP8X4), scales=w2_scales[:, columns],
+                in_=w2_grouped[:, i, :, :].rearrange("p j t -> p (j t)"),
+            )
 
-        for k in range(1, N_CHUNKS + 3):
-            if k + 2 < N_CHUNKS:
-                x_staged[k + 2] = load_rows(x_rows[(k + 2) * CHUNK : (k + 3) * CHUNK, :])
-            if k < N_CHUNKS:
-                flip_chunk(k)
-            if k >= 3:
-                bring_back(k - 3)
-            for i in range(PHASES):
-                for t in range(PACK):
-                    if k - 1 < N_CHUNKS:
-                        first_matmul(k - 1, i, t)
-                    if 0 <= k - 2 < N_CHUNKS:
-                        second_matmul(k - 2, i, t)
-                if k - 1 < N_CHUNKS:
-                    group_g(k - 1, i)
-                    if i == 1:
-                        quantise_g(k - 1, 0)
-            if k < N_CHUNKS:
-                residual(k)
-            if k - 1 < N_CHUNKS:
-                quantise_g(k - 1, 1)
+        w1_codes = consts.tile([P, PHASES * HID], U32, align_bytes=64)
+        w1_scales = consts.tile([P, PHASES * HID], U8, align_bytes=64)
+        w1_flat = lasting.tile([P, PHASES, HID * PACK], BF16, name="flat", align_bytes=64)
+
+        def flip_w1(i, b, copy):
+            flip_bank(w1_staged, w1_flat, b, i, copy)
+            columns = slice(i * HID + b * BANK_ROWS, i * HID + (b + 1) * BANK_ROWS)
+            nc.vector.quantize_mx(
+                out=w1_codes[:, columns].bitcast(FP8X4), scales=w1_scales[:, columns],
+                in_=w1_flat[:, i, b * BANK_ROWS * PACK : (b + 1) * BANK_ROWS * PACK],
+            )
+
+        flips = [(c, i, b) for c in range(N_CHUNKS) for i in range(PHASES) for b in range(CHUNKS[c] // BANK_ROWS)]
+        firsts = [(c, i, t) for c in range(N_CHUNKS) for i in range(PHASES) for t in range(0, PACK, 2)]
+        seconds = list(firsts)
+        backs = [(c, a) for c in range(N_CHUNKS) for a in range(CHUNKS[c] // P)]
+
+        with tc.manual_schedule(engines={mybir.EngineType.PE}):
+            flip(0, 0, 0)
+            flip_w1(0, 0, nc.vector.tensor_copy)
+            flip(0, 1, 0)
+            flip_w1(1, 0, nc.vector.tensor_copy)
+            flip_w1(0, 1, nc.vector.tensor_copy)
+            flip_w1(1, 1, nc.scalar.copy)
+            flips = flips[2:]
+            flipped = {(0, 0): -1, (0, 1): -1}
+            hidden, mixed = {}, {}
+            turn = 0
+            while backs:
+                turn += 1
+                first = second = None
+                if firsts and flipped.get(firsts[0][:2], turn) + FLIP_TO_FIRST <= turn:
+                    first = firsts.pop(0)
+                if seconds and hidden.get(seconds[0][:2], turn) + FIRST_TO_SECOND <= turn:
+                    second = seconds.pop(0)
+                for u in range(2):
+                    if first:
+                        c, i, t = first
+                        first_matmul(c, i, t + u)
+                    if second:
+                        c, i, t = second
+                        second_matmul(c, i, t + u)
+                if turn <= PHASES:
+                    flip_w2(turn - 1)
+                flipping = bool(flips) and (not firsts or flips[0][0] <= firsts[0][0] + 1)
+                if flipping:
+                    c, i, b = flips.pop(0)
+                    flip(c, i, b)
+                    flipped[c, i] = turn
+                at_once = 1 if first or flipping else 2
+                for n in range(at_once):
+                    if backs and mixed.get(backs[0][0], turn) + SECOND_TO_BACK <= turn:
+                        c, a = backs.pop(0)
+                        bring_back(c, a, "flip" if not flips and a % 2 else "back")
+                if first:
+                    c, i, t = first
+                    if t == 2:
+                        group_g(c, i)
+                        quantise_g(c, i)
+                        hidden[c, i] = turn
+                    if i == 0:
+                        residual(c, t)
+                        residual(c, t + 1)
+                if second:
+                    c, i, t = second
+                    if i == 1 and t == 2:
+                        mixed[c] = turn

@@ -32,6 +32,7 @@ DIAGONALS = ((0, 1), (1, 1))
 FLIP_TO_FIRST = 1
 FIRST_TO_SECOND = 2
 SECOND_TO_BACK = 1
+W2_TURNS = (2, 3)
 
 FLOPS = 2 * 2 * PHASES * ROWS * SEG * HID + 4 * ROWS * SEG
 BYTES = 2 * (ROWS * WIDTH + HID * WIDTH + PHASES * SEG * HID + 2 * SEG + 2 * WIDTH + SEG) + 4 * ROWS * WIDTH
@@ -50,27 +51,27 @@ def tile_maskmlp_pa_t_kernel(tc, x, wes1, wes2, wes3, bias1, bias2, bias3, out):
         lasting = ctx.enter_context(tc.tile_pool(name="lasting", bufs=5))
         leaving = ctx.enter_context(tc.tile_pool(name="leaving", bufs=4))
         psum = ctx.enter_context(tc.psum_pool(name="psum", bufs=2))
+        BANKS = {"flip": 1, "hidden": 2, "mixed": 3, "back": 2}
+
+        def bank(shape, dtype, tag):
+            return psum.tile(shape, dtype, name="bank_" + tag, tag=tag, bufs=BANKS[tag])
 
         ident_bf = consts.tile([P, P], BF16)
         make_identity(nc, ident_bf[:])
         ident_f32 = consts.tile([P, P], F32)
         make_identity(nc, ident_f32[:])
 
-        warm = consts.tile([P, 1], F32)
-        nc.vector.memset(warm[:], 0.0)
-        nc.scalar.activation(out=warm[:], in_=warm[:], func=GELU)
-
-        def load_rows(rows):
+        def load_rows(rows, tiles_per_load=FLIPS_PER_BANK):
             pieces = rows.rearrange("r (t w) -> (r t) w", t=PACK).rearrange("(s q) w -> q s w", q=P)
             n_tiles = rows.shape[0] * PACK // P
             staged = staging.tile([P, n_tiles, PIECE], BF16)
-            for s in range(0, n_tiles, FLIPS_PER_BANK):
-                nc.sync.dma_start(out=staged[:, s : s + FLIPS_PER_BANK, :], in_=pieces[:, s : s + FLIPS_PER_BANK, :])
+            for s in range(0, n_tiles, tiles_per_load):
+                nc.sync.dma_start(out=staged[:, s : s + tiles_per_load, :], in_=pieces[:, s : s + tiles_per_load, :])
             return staged
 
-        def flip_bank(staged, flat, b, i, copy):
+        def flip_bank(staged, flat, b, i, copy, tag="flip"):
             by_phase = staged[:].rearrange("q s (j i) -> q s i j", i=PHASES)
-            flipped = psum.tile([P, FLIPS_PER_BANK * P], BF16, tag="flip")
+            flipped = bank([P, FLIPS_PER_BANK * P], BF16, tag)
             for s in range(FLIPS_PER_BANK):
                 nc.tensor.transpose(
                     out=flipped[:, s * P : (s + 1) * P],
@@ -79,12 +80,6 @@ def tile_maskmlp_pa_t_kernel(tc, x, wes1, wes2, wes3, bias1, bias2, bias3, out):
                 )
             columns = slice(b * FLIPS_PER_BANK * P, (b + 1) * FLIPS_PER_BANK * P)
             copy(out=flat[:, i, columns], in_=flipped[:])
-
-        def load_chunk(c):
-            return load_rows(x_rows[FIRST_ROWS[c] : FIRST_ROWS[c] + CHUNKS[c], :])
-
-        x_staged = {0: load_chunk(0)}
-        w1_staged = load_rows(wes1)
 
         small_rows = consts.tile([P, P], BF16)
         nc.vector.memset(small_rows[:], 0.0)
@@ -95,13 +90,23 @@ def tile_maskmlp_pa_t_kernel(tc, x, wes1, wes2, wes3, bias1, bias2, bias3, out):
         w3_bf = consts.tile([P, PACK, PHASES], BF16)
         nc.scalar.dma_start(out=w3_bf[:], in_=w3_pairs.rearrange("(t p) k -> p t k", p=P))
 
+        warm = consts.tile([P, 1], F32)
+        nc.vector.memset(warm[:], 0.0)
+        nc.scalar.activation(out=warm[:], in_=warm[:], func=GELU)
+
+        def load_chunk(c):
+            return load_rows(x_rows[FIRST_ROWS[c] : FIRST_ROWS[c] + CHUNKS[c], :], 2 if c == 0 else FLIPS_PER_BANK)
+
+        x_staged = {0: load_chunk(0)}
+        w1_staged = load_rows(wes1, FLIPS_PER_BANK // 2)
+
         x_staged[1] = load_chunk(1)
         w2_staged = consts.tile([P, PHASES, PACK, HID], BF16)
         for i in range(PHASES):
             block = wes2[i * SEG : (i + 1) * SEG, i * HID : (i + 1) * HID]
             nc.sync.dma_start(out=w2_staged[:, i, :, :], in_=block.rearrange("(t p) h -> p t h", p=P))
 
-        small_ps = psum.tile([P, P], BF16, tag="flip")
+        small_ps = bank([P, P], BF16, "hidden")
         nc.tensor.transpose(out=small_ps[:], in_=small_rows[:], identity=ident_bf[:])
         small_cols = consts.tile([P, 20], F32)
         nc.vector.tensor_copy(out=small_cols[:], in_=small_ps[:, 0:20])
@@ -135,10 +140,10 @@ def tile_maskmlp_pa_t_kernel(tc, x, wes1, wes2, wes3, bias1, bias2, bias3, out):
             xs = double.tile([P, PHASES * CHUNKS[c]], U8, align_bytes=64)
             x_grouped[c], x_codes[c], x_scales[c] = flat, xq, xs
 
-        def flip(c, i, b):
+        def flip(c, i, b, tag="flip"):
             if i == 0 and b == 0:
                 open_chunk(c)
-            flip_bank(x_staged[c], x_grouped[c], b, i, nc.scalar.copy)
+            flip_bank(x_staged[c], x_grouped[c], b, i, nc.scalar.copy, tag)
             if (b + 1) * BANK_ROWS == CHUNKS[c]:
                 columns = slice(i * CHUNKS[c], (i + 1) * CHUNKS[c])
                 nc.vector.quantize_mx(
@@ -175,7 +180,7 @@ def tile_maskmlp_pa_t_kernel(tc, x, wes1, wes2, wes3, bias1, bias2, bias3, out):
                 g_rows[c] = rows
             units = slice(i * HID + t * P, i * HID + (t + 1) * P)
             columns = slice(i * CHUNKS[c], (i + 1) * CHUNKS[c])
-            hidden_ps = psum.tile([P, CHUNKS[c]], F32, tag="hidden")
+            hidden_ps = bank([P, CHUNKS[c]], F32, "hidden")
             nc.tensor.matmul_mx(
                 out=hidden_ps[:],
                 lhsT=w1_codes[:, units].bitcast(FP8X4), lhsT_scale=w1_scales[:, units],
@@ -213,7 +218,7 @@ def tile_maskmlp_pa_t_kernel(tc, x, wes1, wes2, wes3, bias1, bias2, bias3, out):
                 sum_t[c] = sums
             outputs = slice(i * SEG + t * P, i * SEG + (t + 1) * P)
             columns = slice(i * CHUNKS[c], (i + 1) * CHUNKS[c])
-            mixed_ps = psum.tile([P, CHUNKS[c]], F32, tag="mixed")
+            mixed_ps = bank([P, CHUNKS[c]], F32, "mixed")
             nc.tensor.matmul_mx(
                 out=mixed_ps[:],
                 lhsT=w2_codes[:, outputs].bitcast(FP8X4), lhsT_scale=w2_scales[:, outputs],
@@ -232,7 +237,7 @@ def tile_maskmlp_pa_t_kernel(tc, x, wes1, wes2, wes3, bias1, bias2, bias3, out):
             rows = slice(a * P, (a + 1) * P)
             banks = []
             for half in range(2):
-                back_ps = psum.tile([P, PHASES, 2, P], F32, name="back_ps", tag=tag)
+                back_ps = bank([P, PHASES, 2, P], F32, tag)
                 banks.append(back_ps)
                 adds = any(t // 2 == half for t, k in DIAGONALS)
                 for i in range(PHASES):
@@ -261,7 +266,7 @@ def tile_maskmlp_pa_t_kernel(tc, x, wes1, wes2, wes3, bias1, bias2, bias3, out):
 
         def flip_w2(i):
             for half, copy in enumerate((nc.scalar.copy, nc.vector.tensor_copy)):
-                w2_ps = psum.tile([P, 2, PACK, P], BF16, tag="flip")
+                w2_ps = bank([P, 2, PACK, P], BF16, "mixed")
                 for b in range(2):
                     for t in range(PACK):
                         nc.tensor.transpose(
@@ -283,8 +288,8 @@ def tile_maskmlp_pa_t_kernel(tc, x, wes1, wes2, wes3, bias1, bias2, bias3, out):
         w1_scales = consts.tile([P, PHASES * HID], U8, align_bytes=64)
         w1_flat = lasting.tile([P, PHASES, HID * PACK], BF16, name="flat", align_bytes=64)
 
-        def flip_w1(i, b, copy):
-            flip_bank(w1_staged, w1_flat, b, i, copy)
+        def flip_w1(i, b, copy, tag):
+            flip_bank(w1_staged, w1_flat, b, i, copy, tag)
             columns = slice(i * HID + b * BANK_ROWS, i * HID + (b + 1) * BANK_ROWS)
             nc.vector.quantize_mx(
                 out=w1_codes[:, columns].bitcast(FP8X4), scales=w1_scales[:, columns],
@@ -297,12 +302,12 @@ def tile_maskmlp_pa_t_kernel(tc, x, wes1, wes2, wes3, bias1, bias2, bias3, out):
         backs = [(c, a) for c in range(N_CHUNKS) for a in range(CHUNKS[c] // P)]
 
         with tc.manual_schedule(engines={mybir.EngineType.PE}):
-            flip(0, 0, 0)
-            flip_w1(0, 0, nc.vector.tensor_copy)
-            flip(0, 1, 0)
-            flip_w1(1, 0, nc.vector.tensor_copy)
-            flip_w1(0, 1, nc.vector.tensor_copy)
-            flip_w1(1, 1, nc.scalar.copy)
+            flip(0, 0, 0, "flip")
+            flip_w1(0, 0, nc.vector.tensor_copy, "mixed")
+            flip(0, 1, 0, "back")
+            flip_w1(1, 0, nc.vector.tensor_copy, "mixed")
+            flip_w1(0, 1, nc.vector.tensor_copy, "back")
+            flip_w1(1, 1, nc.scalar.copy, "mixed")
             flips = flips[2:]
             flipped = {(0, 0): -1, (0, 1): -1}
             hidden, mixed = {}, {}
@@ -321,8 +326,8 @@ def tile_maskmlp_pa_t_kernel(tc, x, wes1, wes2, wes3, bias1, bias2, bias3, out):
                     if second:
                         c, i, t = second
                         second_matmul(c, i, t + u)
-                if turn <= PHASES:
-                    flip_w2(turn - 1)
+                if turn in W2_TURNS:
+                    flip_w2(W2_TURNS.index(turn))
                 flipping = bool(flips) and (not firsts or flips[0][0] <= firsts[0][0] + 1)
                 if flipping:
                     c, i, b = flips.pop(0)
@@ -332,7 +337,7 @@ def tile_maskmlp_pa_t_kernel(tc, x, wes1, wes2, wes3, bias1, bias2, bias3, out):
                 for n in range(at_once):
                     if backs and mixed.get(backs[0][0], turn) + SECOND_TO_BACK <= turn:
                         c, a = backs.pop(0)
-                        bring_back(c, a, "flip" if not flips and a % 2 else "back")
+                        bring_back(c, a, "hidden" if not firsts and a % 2 else "back")
                 if first:
                     c, i, t = first
                     if t == 2:

from contextlib import ExitStack

import concourse.mybir as mybir
from concourse.masks import make_identity

BF16 = mybir.dt.bfloat16
F32 = mybir.dt.float32
U32 = mybir.dt.uint32
U8 = mybir.dt.uint8
FP8X4 = mybir.dt.float8_e4m3fn_x4
ADD = mybir.AluOpType.add
MULT = mybir.AluOpType.mult
GELU = mybir.ActivationFunctionType.Gelu

P = 128
PACK = 4
PHASES = 2
SEG = 512
HID = 512
WIDTH = PHASES * SEG
ROWS = 8 * 512
CHUNK = 512
CHUNKS = (CHUNK // 2,) + (CHUNK,) * (ROWS // CHUNK - 1) + (CHUNK // 2,)
FIRST_ROWS = tuple(sum(CHUNKS[:c]) for c in range(len(CHUNKS)))
N_CHUNKS = len(CHUNKS)
PIECE = WIDTH // PACK
FLIPS_PER_BANK = 8
BANK_ROWS = FLIPS_PER_BANK * P // PACK

DIAGONALS = ((0, 1), (1, 1))

FLIP_TO_FIRST = 1
FIRST_TO_SECOND = 2
SECOND_TO_BACK = 1
W2_TURNS = (2, 3)

FLOPS = 2 * 2 * PHASES * ROWS * SEG * HID + 4 * ROWS * SEG
BYTES = 2 * (ROWS * WIDTH + HID * WIDTH + PHASES * SEG * HID + 2 * SEG + 2 * WIDTH + SEG) + 4 * ROWS * WIDTH


def tile_maskmlp_pa_t_kernel(tc, x, wes1, wes2, wes3, bias1, bias2, bias3, out):
    nc = tc.nc
    x_rows = x.rearrange("b c l -> (b c) l")
    out_rows = out.rearrange("b c l -> (b c) l")

    with ExitStack() as ctx:
        consts = ctx.enter_context(tc.tile_pool(name="consts", bufs=1))
        staging = ctx.enter_context(tc.tile_pool(name="staging", bufs=3))
        double = ctx.enter_context(tc.tile_pool(name="double", bufs=2))
        triple = ctx.enter_context(tc.tile_pool(name="triple", bufs=3))
        lasting = ctx.enter_context(tc.tile_pool(name="lasting", bufs=5))
        leaving = ctx.enter_context(tc.tile_pool(name="leaving", bufs=4))
        psum = ctx.enter_context(tc.psum_pool(name="psum", bufs=2))
        BANKS = {"flip": 1, "hidden": 2, "mixed": 3, "back": 2}

        def bank(shape, dtype, tag):
            return psum.tile(shape, dtype, name="bank_" + tag, tag=tag, bufs=BANKS[tag])

        ident_bf = consts.tile([P, P], BF16)
        make_identity(nc, ident_bf[:])
        ident_f32 = consts.tile([P, P], F32)
        make_identity(nc, ident_f32[:])

        def load_rows(rows, tiles_per_load=FLIPS_PER_BANK):
            pieces = rows.rearrange("r (t w) -> (r t) w", t=PACK).rearrange("(s q) w -> q s w", q=P)
            n_tiles = rows.shape[0] * PACK // P
            staged = staging.tile([P, n_tiles, PIECE], BF16)
            for s in range(0, n_tiles, tiles_per_load):
                nc.sync.dma_start(out=staged[:, s : s + tiles_per_load, :], in_=pieces[:, s : s + tiles_per_load, :])
            return staged

        def flip_bank(staged, flat, b, i, copy, tag="flip"):
            by_phase = staged[:].rearrange("q s (j i) -> q s i j", i=PHASES)
            flipped = bank([P, FLIPS_PER_BANK * P], BF16, tag)
            for s in range(FLIPS_PER_BANK):
                nc.tensor.transpose(
                    out=flipped[:, s * P : (s + 1) * P],
                    in_=by_phase[:, b * FLIPS_PER_BANK + s, i, :],
                    identity=ident_bf[:],
                )
            columns = slice(b * FLIPS_PER_BANK * P, (b + 1) * FLIPS_PER_BANK * P)
            copy(out=flat[:, i, columns], in_=flipped[:])

        small_rows = consts.tile([P, P], BF16)
        nc.vector.memset(small_rows[:], 0.0)
        nc.scalar.dma_start(out=small_rows[0:8, :], in_=bias1.rearrange("(a p) -> a p", p=P))
        nc.scalar.dma_start(out=small_rows[8:16, :], in_=bias2.rearrange("(a p) -> a p", p=P))
        nc.scalar.dma_start(out=small_rows[16:20, :], in_=bias3.rearrange("(a p) -> a p", p=P))
        w3_pairs = wes3.rearrange("j (jj k) -> (j jj) k", k=PHASES)[0 : SEG * SEG : SEG + 1, :]
        w3_bf = consts.tile([P, PACK, PHASES], BF16)
        nc.scalar.dma_start(out=w3_bf[:], in_=w3_pairs.rearrange("(t p) k -> p t k", p=P))

        warm = consts.tile([P, 1], F32)
        nc.vector.memset(warm[:], 0.0)
        nc.scalar.activation(out=warm[:], in_=warm[:], func=GELU)

        def load_chunk(c):
            return load_rows(x_rows[FIRST_ROWS[c] : FIRST_ROWS[c] + CHUNKS[c], :], 2 if c == 0 else FLIPS_PER_BANK)

        x_staged = {0: load_chunk(0)}
        w1_staged = load_rows(wes1, FLIPS_PER_BANK // 2)

        x_staged[1] = load_chunk(1)
        w2_staged = consts.tile([P, PHASES, PACK, HID], BF16)
        for i in range(PHASES):
            block = wes2[i * SEG : (i + 1) * SEG, i * HID : (i + 1) * HID]
            nc.sync.dma_start(out=w2_staged[:, i, :, :], in_=block.rearrange("(t p) h -> p t h", p=P))

        small_ps = bank([P, P], BF16, "hidden")
        nc.tensor.transpose(out=small_ps[:], in_=small_rows[:], identity=ident_bf[:])
        small_cols = consts.tile([P, 20], F32)
        nc.vector.tensor_copy(out=small_cols[:], in_=small_ps[:, 0:20])
        bias1_col = small_cols[:, 0:8]
        bias23_col = consts.tile([P, PHASES * PACK], F32)
        for i in range(PHASES):
            nc.vector.tensor_add(
                out=bias23_col[:, i * PACK : (i + 1) * PACK],
                in0=small_cols[:, 8 + i * PACK : 8 + (i + 1) * PACK],
                in1=small_cols[:, 16:20],
            )
        w3_col = consts.tile([P, PACK * PHASES], F32)
        nc.vector.tensor_copy(out=w3_col[:], in_=w3_bf[:].rearrange("p t k -> p (t k)"))

        diagonals = {}
        for t, k in DIAGONALS:
            diagonal = consts.tile([P, PHASES, P], BF16, name="diagonal_%d_%d" % (t, k))
            for i in range(PHASES):
                nc.vector.tensor_scalar(
                    out=diagonal[:, i, :], in0=ident_bf[:],
                    scalar1=w3_col[:, 2 * t + k : 2 * t + k + 1], scalar2=None, op0=MULT,
                )
            diagonals[t, k] = diagonal

        x_grouped, x_codes, x_scales, res_t = {}, {}, {}, {}
        g_rows, g_grouped, g_codes, g_scales, sum_t = {}, {}, {}, {}, {}

        def open_chunk(c):
            flat = lasting.tile([P, PHASES, CHUNKS[c] * PACK], BF16, align_bytes=64)
            xq = double.tile([P, PHASES * CHUNKS[c]], U32, align_bytes=64)
            xs = double.tile([P, PHASES * CHUNKS[c]], U8, align_bytes=64)
            x_grouped[c], x_codes[c], x_scales[c] = flat, xq, xs

        def flip(c, i, b, tag="flip"):
            if i == 0 and b == 0:
                open_chunk(c)
            flip_bank(x_staged[c], x_grouped[c], b, i, nc.scalar.copy, tag)
            if (b + 1) * BANK_ROWS == CHUNKS[c]:
                columns = slice(i * CHUNKS[c], (i + 1) * CHUNKS[c])
                nc.vector.quantize_mx(
                    out=x_codes[c][:, columns].bitcast(FP8X4), scales=x_scales[c][:, columns],
                    in_=x_grouped[c][:, i, :],
                )
                if i == 1 and c + 2 < N_CHUNKS:
                    x_staged[c + 2] = load_chunk(c + 2)

        def residual(c, t):
            if t == 0:
                res = triple.tile([P, PACK, CHUNKS[c]], F32)
                res_t[c] = res
            by_tile = x_grouped[c][:].rearrange("p i (r t) -> p i t r", t=PACK)
            w3_even = w3_col[:, 2 * t : 2 * t + 1]
            if (t, 1) in DIAGONALS:
                nc.vector.tensor_scalar(
                    out=res_t[c][:, t, :], in0=by_tile[:, 0, t, :], scalar1=w3_even, scalar2=None, op0=MULT,
                )
            else:
                odd = triple.tile([P, CHUNKS[c]], F32)
                nc.vector.tensor_scalar(
                    out=odd[:], in0=by_tile[:, 1, t, :],
                    scalar1=w3_col[:, 2 * t + 1 : 2 * t + 2], scalar2=None, op0=MULT,
                )
                nc.vector.scalar_tensor_tensor(
                    out=res_t[c][:, t, :], in0=by_tile[:, 0, t, :], scalar=w3_even,
                    in1=odd[:], op0=MULT, op1=ADD,
                )

        def first_matmul(c, i, t):
            if i == 0 and t == 0:
                rows = double.tile([P, PHASES, PACK, CHUNKS[c]], BF16)
                g_rows[c] = rows
            units = slice(i * HID + t * P, i * HID + (t + 1) * P)
            columns = slice(i * CHUNKS[c], (i + 1) * CHUNKS[c])
            hidden_ps = bank([P, CHUNKS[c]], F32, "hidden")
            nc.tensor.matmul_mx(
                out=hidden_ps[:],
                lhsT=w1_codes[:, units].bitcast(FP8X4), lhsT_scale=w1_scales[:, units],
                rhs=x_codes[c][:, columns].bitcast(FP8X4), rhs_scale=x_scales[c][:, columns],
                start=True, stop=True,
            )
            nc.scalar.activation(
                out=g_rows[c][:, i, t, :], in_=hidden_ps[:], func=GELU,
                bias=bias1_col[:, i * PACK + t : i * PACK + t + 1], scale=1.0,
            )

        def group_g(c, i):
            if i == 0:
                grouped = double.tile([P, PHASES, CHUNKS[c] * PACK], BF16, align_bytes=64)
                g_grouped[c] = grouped
            nc.vector.tensor_copy(
                out=g_grouped[c][:, i, :].rearrange("p (c u t) -> p c t u", u=4, t=PACK),
                in_=g_rows[c][:, i, :, :].rearrange("p t (c u) -> p c t u", u=4),
            )

        def quantise_g(c, i):
            if i == 0:
                gq = double.tile([P, PHASES * CHUNKS[c]], U32, align_bytes=64)
                gs = double.tile([P, PHASES * CHUNKS[c]], U8, align_bytes=64)
                g_codes[c], g_scales[c] = gq, gs
            columns = slice(i * CHUNKS[c], (i + 1) * CHUNKS[c])
            nc.vector.quantize_mx(
                out=g_codes[c][:, columns].bitcast(FP8X4), scales=g_scales[c][:, columns],
                in_=g_grouped[c][:, i, :],
            )

        def second_matmul(c, i, t):
            if i == 0 and t == 0:
                sums = double.tile([P, PHASES, PACK, CHUNKS[c]], F32)
                sum_t[c] = sums
            outputs = slice(i * SEG + t * P, i * SEG + (t + 1) * P)
            columns = slice(i * CHUNKS[c], (i + 1) * CHUNKS[c])
            mixed_ps = bank([P, CHUNKS[c]], F32, "mixed")
            nc.tensor.matmul_mx(
                out=mixed_ps[:],
                lhsT=w2_codes[:, outputs].bitcast(FP8X4), lhsT_scale=w2_scales[:, outputs],
                rhs=g_codes[c][:, columns].bitcast(FP8X4), rhs_scale=g_scales[c][:, columns],
                start=True, stop=True,
            )
            bias = bias23_col[:, i * PACK + t : i * PACK + t + 1]
            nc.vector.scalar_tensor_tensor(
                out=sum_t[c][:, i, t, :], in0=mixed_ps[:], scalar=bias,
                in1=res_t[c][:, t, :], op0=ADD, op1=ADD,
            )

        def bring_back(c, a, tag):
            rows_out = leaving.tile([P, WIDTH], F32)
            by_tile = x_grouped[c][:].rearrange("p i (r t) -> p i t r", t=PACK)
            rows = slice(a * P, (a + 1) * P)
            banks = []
            for half in range(2):
                back_ps = bank([P, PHASES, 2, P], F32, tag)
                banks.append(back_ps)
                adds = any(t // 2 == half for t, k in DIAGONALS)
                for i in range(PHASES):
                    for t in range(2):
                        nc.tensor.matmul(
                            out=back_ps[:, i, t, :], lhsT=sum_t[c][:, i, 2 * half + t, rows],
                            rhs=ident_f32[:], is_transpose=True,
                            start=not adds or (i == 0 and t == 0), stop=not adds,
                        )
            for t, k in DIAGONALS:
                nc.tensor.matmul(
                    out=banks[t // 2][:, :, t % 2, :], lhsT=by_tile[:, k, t, rows], rhs=diagonals[t, k][:],
                    start=False, stop=(t, k) == max(d for d in DIAGONALS if d[0] // 2 == t // 2),
                )
            for half in range(2):
                nc.scalar.copy(
                    out=rows_out[:, half * SEG : (half + 1) * SEG].rearrange("p (j i) -> p j i", i=PHASES),
                    in_=banks[half][:].rearrange("p i t j -> p (t j) i"),
                )
            first_row = FIRST_ROWS[c] + a * P
            nc.sync.dma_start(out=out_rows[first_row : first_row + P, :], in_=rows_out[:])

        w2_grouped = consts.tile([P, PHASES, SEG, PACK], BF16, align_bytes=64)
        w2_codes = consts.tile([P, PHASES * SEG], U32, align_bytes=64)
        w2_scales = consts.tile([P, PHASES * SEG], U8, align_bytes=64)

        def flip_w2(i):
            for half, copy in enumerate((nc.scalar.copy, nc.vector.tensor_copy)):
                w2_ps = bank([P, 2, PACK, P], BF16, "mixed")
                for b in range(2):
                    for t in range(PACK):
                        nc.tensor.transpose(
                            out=w2_ps[:, b, t, :],
                            in_=w2_staged[:, i, 2 * half + b, t * P : (t + 1) * P],
                            identity=ident_bf[:],
                        )
                copy(
                    out=w2_grouped[:, i, half * 2 * P : (half + 1) * 2 * P, :].rearrange("p (b j) t -> p b j t", b=2),
                    in_=w2_ps[:].rearrange("p b t j -> p b j t"),
                )
            columns = slice(i * SEG, (i + 1) * SEG)
            nc.vector.quantize_mx(
                out=w2_codes[:, columns].bitcast(FP8X4), scales=w2_scales[:, columns],
                in_=w2_grouped[:, i, :, :].rearrange("p j t -> p (j t)"),
            )

        w1_codes = consts.tile([P, PHASES * HID], U32, align_bytes=64)
        w1_scales = consts.tile([P, PHASES * HID], U8, align_bytes=64)
        w1_flat = lasting.tile([P, PHASES, HID * PACK], BF16, name="flat", align_bytes=64)

        def flip_w1(i, b, copy, tag):
            flip_bank(w1_staged, w1_flat, b, i, copy, tag)
            columns = slice(i * HID + b * BANK_ROWS, i * HID + (b + 1) * BANK_ROWS)
            nc.vector.quantize_mx(
                out=w1_codes[:, columns].bitcast(FP8X4), scales=w1_scales[:, columns],
                in_=w1_flat[:, i, b * BANK_ROWS * PACK : (b + 1) * BANK_ROWS * PACK],
            )

        flips = [(c, i, b) for c in range(N_CHUNKS) for i in range(PHASES) for b in range(CHUNKS[c] // BANK_ROWS)]
        firsts = [(c, i, t) for c in range(N_CHUNKS) for i in range(PHASES) for t in range(0, PACK, 2)]
        seconds = list(firsts)
        backs = [(c, a) for c in range(N_CHUNKS) for a in range(CHUNKS[c] // P)]

        with tc.manual_schedule(engines={mybir.EngineType.PE}):
            flip(0, 0, 0, "flip")
            flip_w1(0, 0, nc.vector.tensor_copy, "mixed")
            flip(0, 1, 0, "back")
            flip_w1(1, 0, nc.vector.tensor_copy, "mixed")
            flip_w1(0, 1, nc.vector.tensor_copy, "back")
            flip_w1(1, 1, nc.scalar.copy, "mixed")
            flips = flips[2:]
            flipped = {(0, 0): -1, (0, 1): -1}
            hidden, mixed = {}, {}
            turn = 0
            while backs:
                turn += 1
                first = second = None
                if firsts and flipped.get(firsts[0][:2], turn) + FLIP_TO_FIRST <= turn:
                    first = firsts.pop(0)
                if seconds and hidden.get(seconds[0][:2], turn) + FIRST_TO_SECOND <= turn:
                    second = seconds.pop(0)
                for u in range(2):
                    if first:
                        c, i, t = first
                        first_matmul(c, i, t + u)
                    if second:
                        c, i, t = second
                        second_matmul(c, i, t + u)
                if turn in W2_TURNS:
                    flip_w2(W2_TURNS.index(turn))
                flipping = bool(flips) and (not firsts or flips[0][0] <= firsts[0][0] + 1)
                if flipping:
                    c, i, b = flips.pop(0)
                    flip(c, i, b)
                    flipped[c, i] = turn
                at_once = 1 if first or flipping else 2
                for n in range(at_once):
                    if backs and mixed.get(backs[0][0], turn) + SECOND_TO_BACK <= turn:
                        c, a = backs.pop(0)
                        bring_back(c, a, "hidden" if not firsts and a % 2 else "back")
                if first:
                    c, i, t = first
                    if t == 2:
                        group_g(c, i)
                        quantise_g(c, i)
                        hidden[c, i] = turn
                    if i == 0:
                        residual(c, t)
                        residual(c, t + 1)
                if second:
                    c, i, t = second
                    if i == 1 and t == 2:
                        mixed[c] = turn
